import numpy as np
import ml_dtypes


def mxq(x, axis, fmt="e4m3"):
    dtype, down = {"e4m3": (ml_dtypes.float8_e4m3fn, 7), "e5m2": (ml_dtypes.float8_e5m2, 14)}[fmt]
    v = np.moveaxis(np.asarray(x, np.float32).astype(ml_dtypes.bfloat16).astype(np.float64), axis, -1)
    blocks = v.reshape(v.shape[:-1] + (-1, 32))
    amax = np.abs(blocks).max(-1, keepdims=True)
    byte = np.maximum(np.where(amax > 0, np.frexp(amax)[1] - 1 + 127, 0) - down, 1)
    scale = np.exp2(byte - 127.0)
    codes = (blocks / scale).astype(np.float32).astype(dtype).astype(np.float64)
    return np.moveaxis((codes * scale).reshape(v.shape), -1, axis)


WIDE = False


def mx_kscale(k):
    if not WIDE:
        return np.ones(k)
    levels = np.array([10, -10, 5, -5, 0])
    a = np.random.permutation(np.resize(levels, k // 512 * 4)).reshape(k // 512, 4)
    idx = np.arange(k)
    return np.exp2(a[idx // 512, idx % 128 // 32])


BF16 = ml_dtypes.bfloat16


def bf(x):
    return np.asarray(x, np.float32).astype(BF16)


def f64(x):
    return np.asarray(x).astype(np.float64)


B, H = 4096, 512
EPS = 1e-5
NUM_GROUPS = 4


def sigmoid(v):
    return 1.0 / (1.0 + np.exp(-v))


def _group_norm(z, weight, bias):
    n, ch = z.shape
    zg = z.reshape(n, NUM_GROUPS, ch // NUM_GROUPS)
    mean = zg.mean(axis=-1, keepdims=True)
    var = zg.var(axis=-1, keepdims=True)
    zn = (zg - mean) / np.sqrt(var + EPS)
    return zn.reshape(n, ch) * weight + bias


def setup_inputs():
    s = mx_kscale(H)
    return {"x": bf(np.random.standard_normal((1, B, H))),
            "h": bf(np.random.standard_normal((B, H)) * s),
            "c": bf(np.random.standard_normal((B, H))),
            "W": bf(np.random.uniform(-1.0, 1.0, (NUM_GROUPS * H, H)) / np.sqrt(H) / s[None, :]),
            "b": bf(np.random.standard_normal(NUM_GROUPS * H) * 0.3),
            "gn_weight": bf(1.0 + 0.1 * np.random.standard_normal(NUM_GROUPS * H)),
            "gn_bias": bf(0.1 * np.random.standard_normal(NUM_GROUPS * H))}


def reference(x, h, c, W, b, gn_weight, gn_bias):
    lin = (mxq(f64(h), 1, "e4m3") @ mxq(f64(W), 1, "e4m3").T) + f64(b)
    z = _group_norm(lin, f64(gn_weight), f64(gn_bias))
    i, f, o, g = np.split(z, NUM_GROUPS, axis=1)
    c_new = sigmoid(f) * f64(c) + sigmoid(i) * np.tanh(g)
    h_new = sigmoid(o) * np.tanh(c_new)
    return (h_new, c_new)

@@ -1,0 +1,331 @@
+from contextlib import ExitStack
+
+import concourse.mybir as mybir
+from concourse.masks import make_identity
+
+F32 = mybir.dt.float32
+BF16 = mybir.dt.bfloat16
+U32 = mybir.dt.uint32
+U8 = mybir.dt.uint8
+FP8X4 = mybir.dt.float8_e4m3fn_x4
+ALU = mybir.AluOpType
+ACT = mybir.ActivationFunctionType
+
+P = 128
+B = 4096
+H = 512
+G = 4
+EPS = 1e-5
+A = 4
+S = B // (A * P)
+NU = S * G
+GATE_ORDER = [0, 3, 1, 2]
+FUNCS = [ACT.Sigmoid, ACT.Sigmoid, ACT.Sigmoid, ACT.Tanh]
+
+FLOPS = 2 * B * G * H * H
+BYTES = 2 * (2 * B * H + G * H * H + 3 * G * H) + 4 * 2 * B * H
+
+L_SQ = 4
+L_VE = 9
+L_P3 = 10
+L_TF = 15
+L_P2 = 8
+L_D = 32
+L_H = 1
+P2_ON_VECTOR = (0, 1)
+
+
+def tile_lstmcell2_t_kernel(tc, x, h, c, W, b, gn_weight, gn_bias, out_0, out_1):
+    nc = tc.nc
+    h_v = h.rearrange("(s p a) k -> s p (a k)", p=P, a=A)
+    c_v = c.rearrange("(s p a) k -> s p (a k)", p=P, a=A)
+    ho_v = out_0.rearrange("(s p a) k -> s p (a k)", p=P, a=A)
+    co_v = out_1.rearrange("(s p a) k -> s p (a k)", p=P, a=A)
+    w_v = W.rearrange("(g t p) k -> g p t k", p=P, t=4)
+
+    with ExitStack() as ctx:
+        const = ctx.enter_context(tc.tile_pool(name="const", bufs=1))
+        ps_y = ctx.enter_context(tc.psum_pool(name="ps_y", bufs=3))
+        ps_n = ctx.enter_context(tc.psum_pool(name="ps_n", bufs=2))
+        ps_k = ctx.enter_context(tc.psum_pool(name="ps_k", bufs=3))
+        hin = ctx.enter_context(tc.tile_pool(name="hin", bufs=3))
+        cin = ctx.enter_context(tc.tile_pool(name="cin", bufs=5))
+        hq = ctx.enter_context(tc.tile_pool(name="hq", bufs=2))
+
+        warm = const.tile([P, 1], F32)
+        nc.vector.memset(warm[:], 0.0)
+        warm2 = const.tile([P, 1], F32)
+        nc.scalar.activation(out=warm2[:], in_=warm[:], func=ACT.Sigmoid)
+
+        ident = const.tile([P, P], F32)
+        make_identity(nc, ident[:])
+        negh = const.tile([P, A], F32)
+        nc.vector.memset(negh[:], -0.5)
+
+        w_codes = const.tile([P, G * H], U32, align_bytes=64)
+        w_scales = const.tile([P, G * H], U8, align_bytes=64)
+        b_bc = const.tile([P, G * H], BF16)
+        gwb = const.tile([P, 32], F32)
+
+        h_raw = {}
+        c_raw = {}
+        h_codes = {}
+        h_scales = {}
+
+        def load(s):
+            hr = hin.tile([P, A * H], BF16, tag="h_raw")
+            nc.sync.dma_start(out=hr[:], in_=h_v[s])
+            h_raw[s] = hr
+
+        def load_c(s):
+            cr = cin.tile([P, A * H], BF16, tag="c_raw")
+            nc.sync.dma_start(out=cr[:], in_=c_v[s])
+            c_raw[s] = cr
+
+        def words_to_grouped(raw, grouped, n_tiles, engines):
+            g32 = grouped.bitcast(F32).rearrange("p (a c u) -> p a c u", c=P, u=2)
+            for pair in range(n_tiles // 2):
+                xt = ps_n.tile([P, H], F32, tag="nT")
+                xv = xt[:].rearrange("p (a u c) -> p a u c", a=2, u=2)
+                for a in range(2):
+                    t = 2 * pair + a
+                    words = raw[:, t * H : (t + 1) * H].bitcast(F32)
+                    for u in range(2):
+                        nc.tensor.transpose(xv[:, a, u, :], words[:, u * P : (u + 1) * P], ident[:])
+                src = xt[:].rearrange("p (a u c) -> p a c u", a=2, u=2)
+                dst = g32[:, 2 * pair : 2 * pair + 2, :, :]
+                if engines[pair % len(engines)] == "v":
+                    nc.vector.tensor_copy(out=dst, in_=src)
+                else:
+                    nc.scalar.copy(out=dst, in_=src)
+
+        def prep_h(s):
+            hg = hq.tile([P, A * P * 4], BF16, tag="h_grouped", align_bytes=64)
+            words_to_grouped(h_raw[s][:], hg[:], A, ["v"])
+            hc = hq.tile([P, A * P], U32, tag="h_codes", align_bytes=64)
+            hs = hq.tile([P, A * P], U8, tag="h_scales", align_bytes=64)
+            nc.vector.quantize_mx(out=hc[:].bitcast(FP8X4), scales=hs[:], in_=hg[:])
+            h_codes[s] = hc
+            h_scales[s] = hs
+
+        load(0)
+        with tc.tile_pool(name="wprep", bufs=1) as wprep:
+            w_raw = wprep.tile([P, G * 4 * H], BF16)
+            for g in GATE_ORDER:
+                nc.sync.dma_start(
+                    out=w_raw[:, g * 4 * H : (g + 1) * 4 * H].rearrange("p (t k) -> p t k", k=H),
+                    in_=w_v[g],
+                )
+            nc.scalar.dma_start(out=b_bc[:], in_=b.partition_broadcast(P))
+            rows16 = wprep.tile([P, P], BF16)
+            nc.vector.memset(rows16[:], 0.0)
+            nc.scalar.dma_start(out=rows16[0:16, :], in_=gn_weight.rearrange("(j c) -> j c", c=P))
+            nc.scalar.dma_start(out=rows16[16:32, :], in_=gn_bias.rearrange("(j c) -> j c", c=P))
+            load_c(0)
+            load(1)
+            rows32 = wprep.tile([P, P], F32)
+            nc.vector.tensor_copy(out=rows32[:], in_=rows16[:])
+            prep_h(0)
+            w_grouped = wprep.tile([P, G * H * 4], BF16, align_bytes=64)
+            for g in GATE_ORDER:
+                words_to_grouped(
+                    w_raw[:, g * 4 * H : (g + 1) * 4 * H],
+                    w_grouped[:, g * 4 * H : (g + 1) * 4 * H],
+                    4,
+                    ["v", "s"],
+                )
+                nc.vector.quantize_mx(
+                    out=w_codes[:, g * H : (g + 1) * H].bitcast(FP8X4),
+                    scales=w_scales[:, g * H : (g + 1) * H],
+                    in_=w_grouped[:, g * H * 4 : (g + 1) * H * 4],
+                )
+            colsT = ps_n.tile([P, H], F32, tag="nT")
+            nc.tensor.transpose(colsT[:, 0:P], rows32[:], ident[:])
+            nc.vector.tensor_copy(out=gwb[:], in_=colsT[:, 0:32])
+
+        work = ctx.enter_context(tc.tile_pool(name="work", bufs=2))
+        linp = ctx.enter_context(tc.tile_pool(name="linp", bufs=5))
+        gtp = ctx.enter_context(tc.tile_pool(name="gtp", bufs=7))
+        small = ctx.enter_context(tc.tile_pool(name="small", bufs=8))
+        outp = ctx.enter_context(tc.tile_pool(name="outp", bufs=2))
+
+        lin = {}
+        s1 = {}
+        nm = {}
+        s2 = {}
+        ve = {}
+        rstd = {}
+        gT = {}
+        fin = {}
+
+        def mx(u, a):
+            s = u // G
+            g = GATE_ORDER[u % G]
+            if a == 0:
+                lt = linp.tile([P, A, H], F32, tag="lin")
+                lin[u] = lt
+                t1 = small.tile([P, A], F32, tag="s1")
+                s1[u] = t1
+            gc = slice(g * H, (g + 1) * H)
+            rows = slice(a * P, (a + 1) * P)
+            y = ps_y.tile([P, H], F32, tag="y")
+            nc.tensor.matmul_mx(
+                out=y[:],
+                lhsT=h_codes[s][:, rows].bitcast(FP8X4),
+                lhsT_scale=h_scales[s][:, rows],
+                rhs=w_codes[:, gc].bitcast(FP8X4),
+                rhs_scale=w_scales[:, gc],
+                start=True,
+                stop=True,
+            )
+            nc.vector.scalar_tensor_tensor(
+                out=lin[u][:, a, :],
+                in0=y[:],
+                scalar=1.0,
+                in1=b_bc[:, gc],
+                op0=ALU.mult,
+                op1=ALU.add,
+                accum_out=s1[u][:, a : a + 1],
+            )
+            if a == A - 1:
+                t2 = small.tile([P, A], F32, tag="nm")
+                nm[u] = t2
+                nc.vector.tensor_scalar(
+                    out=t2[:], in0=s1[u][:], scalar1=-1.0 / H, scalar2=None, op0=ALU.mult
+                )
+
+        def sq(u, a):
+            if a == 0:
+                t3 = small.tile([P, A], F32, tag="s2")
+                s2[u] = t3
+            junk = work.tile([P, H], F32, tag="junk")
+            nc.scalar.activation(
+                out=junk[:],
+                in_=lin[u][:, a, :],
+                func=ACT.Square,
+                bias=nm[u][:, a : a + 1],
+                accum_out=s2[u][:, a : a + 1],
+            )
+
+        def var_eps(u):
+            t4 = small.tile([P, A], F32, tag="ve")
+            ve[u] = t4
+            nc.vector.tensor_scalar(
+                out=t4[:], in0=s2[u][:], scalar1=1.0 / H, scalar2=EPS, op0=ALU.mult, op1=ALU.add
+            )
+
+        def p3(u, a):
+            if a == 0:
+                t5 = small.tile([P, A], F32, tag="rstd")
+                rstd[u] = t5
+                nc.gpsimd.tensor_tensor(out=t5[:], in0=ve[u][:], in1=negh[:], op=ALU.pow)
+            nc.gpsimd.tensor_scalar(
+                out=lin[u][:, a, :],
+                in0=lin[u][:, a, :],
+                scalar1=nm[u][:, a : a + 1],
+                scalar2=rstd[u][:, a : a + 1],
+                op0=ALU.add,
+                op1=ALU.mult,
+            )
+
+        def tf(u, j):
+            g = GATE_ORDER[u % G]
+            if j == 0:
+                gt = gtp.tile([P, 4, A * P], F32, tag="gT")
+                gT[u] = gt
+            nT = ps_n.tile([P, H], F32, tag="nT")
+            for a in range(A):
+                nc.tensor.transpose(
+                    nT[:, a * P : (a + 1) * P], lin[u][:, a, j * P : (j + 1) * P], ident[:]
+                )
+            jb = g * 4 + j
+            nc.scalar.activation(
+                out=gT[u][:, j, :],
+                in_=nT[:],
+                func=FUNCS[g],
+                scale=gwb[:, jb : jb + 1],
+                bias=gwb[:, 16 + jb : 17 + jb],
+            )
+
+        def p2(s, j):
+            gi = gT[G * s][:, j, :]
+            gg = gT[G * s + 1][:, j, :]
+            if j in P2_ON_VECTOR:
+                nc.vector.tensor_tensor(out=gi, in0=gi, in1=gg, op=ALU.mult)
+            else:
+                nc.gpsimd.tensor_tensor(out=gi, in0=gi, in1=gg, op=ALU.mult)
+
+        def back(src, a):
+            bk = ps_k.tile([P, H], F32, tag="bk")
+            for j in range(4):
+                nc.tensor.transpose(
+                    bk[:, j * P : (j + 1) * P], src[:, j, a * P : (a + 1) * P], ident[:]
+                )
+            return bk
+
+        def d(s, a, k):
+            cols = slice(a * H, (a + 1) * H)
+            if k == 0:
+                if a == 0:
+                    co = outp.tile([P, A * H], F32, tag="c_out")
+                    fin["c_out"] = co
+                sf = back(gT[G * s + 2], a)
+                p1 = work.tile([P, H], F32, tag="p1")
+                fin["p1"] = p1
+                nc.vector.tensor_tensor(out=p1[:], in0=sf[:], in1=c_raw[s][:, cols], op=ALU.mult)
+            if k == 1:
+                pp = back(gT[G * s], a)
+                nc.vector.tensor_tensor(
+                    out=fin["c_out"][:, cols], in0=pp[:], in1=fin["p1"][:], op=ALU.add
+                )
+            if k == 2:
+                so = back(gT[G * s + 3], a)
+                fin["so", a] = so
+                tcn = work.tile([P, H], F32, tag="tc")
+                fin["tc", a] = tcn
+                nc.scalar.activation(out=tcn[:], in_=fin["c_out"][:, cols], func=ACT.Tanh)
+                if a == A - 1:
+                    nc.sync.dma_start(out=co_v[s], in_=fin["c_out"][:])
+
+        def dh(s, a):
+            cols = slice(a * H, (a + 1) * H)
+            if a == 0:
+                ho = outp.tile([P, A * H], F32, tag="h_out")
+                fin["h_out"] = ho
+            nc.vector.tensor_tensor(
+                out=fin["h_out"][:, cols], in0=fin["so", a][:], in1=fin["tc", a][:], op=ALU.mult
+            )
+            if a == A - 1:
+                nc.sync.dma_start(out=ho_v[s], in_=fin["h_out"][:])
+
+        for q in range(16 * S + L_D + 24):
+            u, a = divmod(q, 4)
+            if u < NU:
+                mx(u, a)
+            if q % 16 == 2 and q // 16 + 2 < S:
+                load(q // 16 + 2)
+            if q % 16 == 4 and q // 16 + 1 < S:
+                load_c(q // 16 + 1)
+            if q % 16 == 6 and q // 16 + 1 < S:
+                prep_h(q // 16 + 1)
+            u, a = divmod(q - L_TF, 4)
+            if 0 <= u < NU:
+                tf(u, a)
+            s, r = divmod(q - L_D, 16)
+            if 0 <= s < S:
+                d(s, r // 4, r % 4)
+            s, r = divmod(q - L_D - 3 - L_H, 16)
+            if 0 <= s < S and r % 4 == 0:
+                dh(s, r // 4)
+            u, a = divmod(q - L_SQ, 4)
+            if 0 <= u < NU:
+                sq(u, a)
+            u, a = divmod(q - L_VE, 4)
+            if 0 <= u < NU and a == 0:
+                var_eps(u)
+            u, a = divmod(q - L_P3, 4)
+            if 0 <= u < NU:
+                p3(u, a)
+            s, r = divmod(q - L_TF - L_P2, 16)
+            if 0 <= s < S and r < 4:
+                p2(s, r)

@@ -33,6 +33,8 @@ L_P2 = 8
 L_D = 32
 L_H = 1
 P2_ON_VECTOR = (0, 1)
+MXB = 2
+DUP = ()
 
 
 def tile_lstmcell2_t_kernel(tc, x, h, c, W, b, gn_weight, gn_bias, out_0, out_1):
@@ -44,13 +46,21 @@ def tile_lstmcell2_t_kernel(tc, x, h, c, W, b, gn_weight, gn_bias, out_0, out_1)
     w_v = W.rearrange("(g t p) k -> g p t k", p=P, t=4)
 
     with ExitStack() as ctx:
+        ctx.enter_context(tc.manual_schedule())
         const = ctx.enter_context(tc.tile_pool(name="const", bufs=1))
-        ps_y = ctx.enter_context(tc.psum_pool(name="ps_y", bufs=3))
-        ps_n = ctx.enter_context(tc.psum_pool(name="ps_n", bufs=2))
+        ps_y = ctx.enter_context(tc.psum_pool(name="ps_y", bufs=2))
+        ps_n = ctx.enter_context(tc.psum_pool(name="ps_n", bufs=3))
         ps_k = ctx.enter_context(tc.psum_pool(name="ps_k", bufs=3))
-        hin = ctx.enter_context(tc.tile_pool(name="hin", bufs=3))
-        cin = ctx.enter_context(tc.tile_pool(name="cin", bufs=5))
+        hin = ctx.enter_context(tc.tile_pool(name="hin", bufs=2))
+        cin = ctx.enter_context(tc.tile_pool(name="cin", bufs=3))
         hq = ctx.enter_context(tc.tile_pool(name="hq", bufs=2))
+        wraw = ctx.enter_context(tc.tile_pool(name="wraw", bufs=4))
+        wgrp = ctx.enter_context(tc.tile_pool(name="wgrp", bufs=2))
+        work = ctx.enter_context(tc.tile_pool(name="work", bufs=2))
+        linp = ctx.enter_context(tc.tile_pool(name="linp", bufs=5))
+        gtp = ctx.enter_context(tc.tile_pool(name="gtp", bufs=7))
+        small = ctx.enter_context(tc.tile_pool(name="small", bufs=8))
+        outp = ctx.enter_context(tc.tile_pool(name="outp", bufs=2))
 
         warm = const.tile([P, 1], F32)
         nc.vector.memset(warm[:], 0.0)
@@ -66,9 +76,12 @@ def tile_lstmcell2_t_kernel(tc, x, h, c, W, b, gn_weight, gn_bias, out_0, out_1)
         w_scales = const.tile([P, G * H], U8, align_bytes=64)
         b_bc = const.tile([P, G * H], BF16)
         gwb = const.tile([P, 32], F32)
+        rows16 = const.tile([P, P], BF16)
+        rows32 = const.tile([P, P], F32)
 
         h_raw = {}
         c_raw = {}
+        w_raw = {}
         h_codes = {}
         h_scales = {}
 
@@ -81,6 +94,11 @@ def tile_lstmcell2_t_kernel(tc, x, h, c, W, b, gn_weight, gn_bias, out_0, out_1)
             cr = cin.tile([P, A * H], BF16, tag="c_raw")
             nc.sync.dma_start(out=cr[:], in_=c_v[s])
             c_raw[s] = cr
+
+        def load_w(g):
+            wr = wraw.tile([P, 4 * H], BF16, tag="w_raw")
+            nc.sync.dma_start(out=wr[:].rearrange("p (t k) -> p t k", k=H), in_=w_v[g])
+            w_raw[g] = wr
 
         def words_to_grouped(raw, grouped, n_tiles, engines):
             g32 = grouped.bitcast(F32).rearrange("p (a c u) -> p a c u", c=P, u=2)
@@ -108,46 +126,32 @@ def tile_lstmcell2_t_kernel(tc, x, h, c, W, b, gn_weight, gn_bias, out_0, out_1)
             h_codes[s] = hc
             h_scales[s] = hs
 
-        load(0)
-        with tc.tile_pool(name="wprep", bufs=1) as wprep:
-            w_raw = wprep.tile([P, G * 4 * H], BF16)
-            for g in GATE_ORDER:
-                nc.sync.dma_start(
-                    out=w_raw[:, g * 4 * H : (g + 1) * 4 * H].rearrange("p (t k) -> p t k", k=H),
-                    in_=w_v[g],
-                )
-            nc.scalar.dma_start(out=b_bc[:], in_=b.partition_broadcast(P))
-            rows16 = wprep.tile([P, P], BF16)
-            nc.vector.memset(rows16[:], 0.0)
-            nc.scalar.dma_start(out=rows16[0:16, :], in_=gn_weight.rearrange("(j c) -> j c", c=P))
-            nc.scalar.dma_start(out=rows16[16:32, :], in_=gn_bias.rearrange("(j c) -> j c", c=P))
-            load_c(0)
-            load(1)
-            rows32 = wprep.tile([P, P], F32)
+        def prep_w(g):
+            wg = wgrp.tile([P, H * 4], BF16, tag="w_grouped", align_bytes=64)
+            words_to_grouped(w_raw[g][:], wg[:], 4, ["v", "s"])
+            nc.vector.quantize_mx(
+                out=w_codes[:, g * H : (g + 1) * H].bitcast(FP8X4),
+                scales=w_scales[:, g * H : (g + 1) * H],
+                in_=wg[:],
+            )
+
+        def prep_gwb():
             nc.vector.tensor_copy(out=rows32[:], in_=rows16[:])
-            prep_h(0)
-            w_grouped = wprep.tile([P, G * H * 4], BF16, align_bytes=64)
-            for g in GATE_ORDER:
-                words_to_grouped(
-                    w_raw[:, g * 4 * H : (g + 1) * 4 * H],
-                    w_grouped[:, g * 4 * H : (g + 1) * 4 * H],
-                    4,
-                    ["v", "s"],
-                )
-                nc.vector.quantize_mx(
-                    out=w_codes[:, g * H : (g + 1) * H].bitcast(FP8X4),
-                    scales=w_scales[:, g * H : (g + 1) * H],
-                    in_=w_grouped[:, g * H * 4 : (g + 1) * H * 4],
-                )
             colsT = ps_n.tile([P, H], F32, tag="nT")
             nc.tensor.transpose(colsT[:, 0:P], rows32[:], ident[:])
             nc.vector.tensor_copy(out=gwb[:], in_=colsT[:, 0:32])
 
-        work = ctx.enter_context(tc.tile_pool(name="work", bufs=2))
-        linp = ctx.enter_context(tc.tile_pool(name="linp", bufs=5))
-        gtp = ctx.enter_context(tc.tile_pool(name="gtp", bufs=7))
-        small = ctx.enter_context(tc.tile_pool(name="small", bufs=8))
-        outp = ctx.enter_context(tc.tile_pool(name="outp", bufs=2))
+        nc.vector.memset(rows16[:], 0.0)
+        load(0)
+        load_w(GATE_ORDER[0])
+        nc.scalar.dma_start(out=b_bc[:], in_=b.partition_broadcast(P))
+        nc.scalar.dma_start(out=rows16[0:16, :], in_=gn_weight.rearrange("(j c) -> j c", c=P))
+        nc.scalar.dma_start(out=rows16[16:32, :], in_=gn_bias.rearrange("(j c) -> j c", c=P))
+        for g in GATE_ORDER[1:]:
+            load_w(g)
+        load(1)
+        prep_h(0)
+        prep_w(GATE_ORDER[0])
 
         lin = {}
         s1 = {}
@@ -158,36 +162,41 @@ def tile_lstmcell2_t_kernel(tc, x, h, c, W, b, gn_weight, gn_bias, out_0, out_1)
         gT = {}
         fin = {}
 
-        def mx(u, a):
+        def mx(u, tiles):
             s = u // G
             g = GATE_ORDER[u % G]
-            if a == 0:
+            gc = slice(g * H, (g + 1) * H)
+            if tiles[0] == 0:
                 lt = linp.tile([P, A, H], F32, tag="lin")
                 lin[u] = lt
                 t1 = small.tile([P, A], F32, tag="s1")
                 s1[u] = t1
-            gc = slice(g * H, (g + 1) * H)
-            rows = slice(a * P, (a + 1) * P)
-            y = ps_y.tile([P, H], F32, tag="y")
-            nc.tensor.matmul_mx(
-                out=y[:],
-                lhsT=h_codes[s][:, rows].bitcast(FP8X4),
-                lhsT_scale=h_scales[s][:, rows],
-                rhs=w_codes[:, gc].bitcast(FP8X4),
-                rhs_scale=w_scales[:, gc],
-                start=True,
-                stop=True,
-            )
-            nc.vector.scalar_tensor_tensor(
-                out=lin[u][:, a, :],
-                in0=y[:],
-                scalar=1.0,
-                in1=b_bc[:, gc],
-                op0=ALU.mult,
-                op1=ALU.add,
-                accum_out=s1[u][:, a : a + 1],
-            )
-            if a == A - 1:
+            banks = []
+            for a in tiles:
+                rows = slice(a * P, (a + 1) * P)
+                y = ps_y.tile([P, H], F32, tag="y")
+                banks.append(y)
+                for rep in range(2 if a in DUP else 1):
+                    nc.tensor.matmul_mx(
+                        out=y[:],
+                        lhsT=h_codes[s][:, rows].bitcast(FP8X4),
+                        lhsT_scale=h_scales[s][:, rows],
+                        rhs=w_codes[:, gc].bitcast(FP8X4),
+                        rhs_scale=w_scales[:, gc],
+                        start=True,
+                        stop=True,
+                    )
+            for a, y in zip(tiles, banks):
+                nc.vector.scalar_tensor_tensor(
+                    out=lin[u][:, a, :],
+                    in0=y[:],
+                    scalar=1.0,
+                    in1=b_bc[:, gc],
+                    op0=ALU.mult,
+                    op1=ALU.add,
+                    accum_out=s1[u][:, a : a + 1],
+                )
+            if tiles[-1] == A - 1:
                 t2 = small.tile([P, A], F32, tag="nm")
                 nm[u] = t2
                 nc.vector.tensor_scalar(
@@ -300,12 +309,16 @@ def tile_lstmcell2_t_kernel(tc, x, h, c, W, b, gn_weight, gn_bias, out_0, out_1)
 
         for q in range(16 * S + L_D + 24):
             u, a = divmod(q, 4)
-            if u < NU:
-                mx(u, a)
-            if q % 16 == 2 and q // 16 + 2 < S:
+            if u < NU and a % MXB == 0:
+                mx(u, list(range(a, a + MXB)))
+            if q in (1, 5, 9):
+                prep_w(GATE_ORDER[q // 4 + 1])
+            if q == 11:
+                prep_gwb()
+            if q % 16 == 10 and q // 16 + 2 < S:
                 load(q // 16 + 2)
-            if q % 16 == 4 and q // 16 + 1 < S:
-                load_c(q // 16 + 1)
+            if q % 16 == 0 and q // 16 < S:
+                load_c(q // 16)
             if q % 16 == 6 and q // 16 + 1 < S:
                 prep_h(q // 16 + 1)
             u, a = divmod(q - L_TF, 4)

@@ -34,7 +34,7 @@ L_D = 32
 L_H = 1
 P2_ON_VECTOR = (0, 1)
 MXB = 2
-DUP = ()
+DUP = (0, 1, 2, 3)
 
 
 def tile_lstmcell2_t_kernel(tc, x, h, c, W, b, gn_weight, gn_bias, out_0, out_1):

@@ -26,15 +26,14 @@ FLOPS = 2 * B * G * H * H
 BYTES = 2 * (2 * B * H + G * H * H + 3 * G * H) + 4 * 2 * B * H
 
 L_SQ = 4
-L_VE = 9
 L_P3 = 10
 L_TF = 15
 L_P2 = 8
-L_D = 32
+L_D = 28
+L_D2 = 33
 L_H = 1
-P2_ON_VECTOR = (0, 1)
 MXB = 2
-DUP = (0, 1, 2, 3)
+DUP = ()
 
 
 def tile_lstmcell2_t_kernel(tc, x, h, c, W, b, gn_weight, gn_bias, out_0, out_1):
@@ -56,7 +55,7 @@ def tile_lstmcell2_t_kernel(tc, x, h, c, W, b, gn_weight, gn_bias, out_0, out_1)
         hq = ctx.enter_context(tc.tile_pool(name="hq", bufs=2))
         wraw = ctx.enter_context(tc.tile_pool(name="wraw", bufs=4))
         wgrp = ctx.enter_context(tc.tile_pool(name="wgrp", bufs=2))
-        work = ctx.enter_context(tc.tile_pool(name="work", bufs=2))
+        work = ctx.enter_context(tc.tile_pool(name="work", bufs=3))
         linp = ctx.enter_context(tc.tile_pool(name="linp", bufs=5))
         gtp = ctx.enter_context(tc.tile_pool(name="gtp", bufs=7))
         small = ctx.enter_context(tc.tile_pool(name="small", bufs=8))
@@ -71,6 +70,8 @@ def tile_lstmcell2_t_kernel(tc, x, h, c, W, b, gn_weight, gn_bias, out_0, out_1)
         make_identity(nc, ident[:])
         negh = const.tile([P, A], F32)
         nc.vector.memset(negh[:], -0.5)
+        eps_t = const.tile([P, 1], F32)
+        nc.vector.memset(eps_t[:], EPS)
 
         w_codes = const.tile([P, G * H], U32, align_bytes=64)
         w_scales = const.tile([P, G * H], U8, align_bytes=64)
@@ -215,13 +216,12 @@ def tile_lstmcell2_t_kernel(tc, x, h, c, W, b, gn_weight, gn_bias, out_0, out_1)
                 bias=nm[u][:, a : a + 1],
                 accum_out=s2[u][:, a : a + 1],
             )
-
-        def var_eps(u):
-            t4 = small.tile([P, A], F32, tag="ve")
-            ve[u] = t4
-            nc.vector.tensor_scalar(
-                out=t4[:], in0=s2[u][:], scalar1=1.0 / H, scalar2=EPS, op0=ALU.mult, op1=ALU.add
-            )
+            if a == A - 1:
+                t4 = small.tile([P, A], F32, tag="ve")
+                ve[u] = t4
+                nc.scalar.activation(
+                    out=t4[:], in_=s2[u][:], func=ACT.Identity, scale=1.0 / H, bias=eps_t[:]
+                )
 
         def p3(u, a):
             if a == 0:
@@ -259,10 +259,7 @@ def tile_lstmcell2_t_kernel(tc, x, h, c, W, b, gn_weight, gn_bias, out_0, out_1)
         def p2(s, j):
             gi = gT[G * s][:, j, :]
             gg = gT[G * s + 1][:, j, :]
-            if j in P2_ON_VECTOR:
-                nc.vector.tensor_tensor(out=gi, in0=gi, in1=gg, op=ALU.mult)
-            else:
-                nc.gpsimd.tensor_tensor(out=gi, in0=gi, in1=gg, op=ALU.mult)
+            nc.vector.tensor_tensor(out=gi, in0=gi, in1=gg, op=ALU.mult)
 
         def back(src, a):
             bk = ps_k.tile([P, H], F32, tag="bk")
@@ -288,13 +285,17 @@ def tile_lstmcell2_t_kernel(tc, x, h, c, W, b, gn_weight, gn_bias, out_0, out_1)
                     out=fin["c_out"][:, cols], in0=pp[:], in1=fin["p1"][:], op=ALU.add
                 )
             if k == 2:
-                so = back(gT[G * s + 3], a)
-                fin["so", a] = so
                 tcn = work.tile([P, H], F32, tag="tc")
                 fin["tc", a] = tcn
                 nc.scalar.activation(out=tcn[:], in_=fin["c_out"][:, cols], func=ACT.Tanh)
-                if a == A - 1:
+                if s == S - 1:
+                    nc.sync.dma_start(out=co_v[s][:, cols], in_=fin["c_out"][:, cols])
+                elif a == A - 1:
                     nc.sync.dma_start(out=co_v[s], in_=fin["c_out"][:])
+
+        def dso(s, a):
+            so = back(gT[G * s + 3], a)
+            fin["so", a] = so
 
         def dh(s, a):
             cols = slice(a * H, (a + 1) * H)
@@ -304,10 +305,12 @@ def tile_lstmcell2_t_kernel(tc, x, h, c, W, b, gn_weight, gn_bias, out_0, out_1)
             nc.vector.tensor_tensor(
                 out=fin["h_out"][:, cols], in0=fin["so", a][:], in1=fin["tc", a][:], op=ALU.mult
             )
-            if a == A - 1:
+            if s == S - 1:
+                nc.sync.dma_start(out=ho_v[s][:, cols], in_=fin["h_out"][:, cols])
+            elif a == A - 1:
                 nc.sync.dma_start(out=ho_v[s], in_=fin["h_out"][:])
 
-        for q in range(16 * S + L_D + 24):
+        for q in range(16 * S + L_D2 + 24):
             u, a = divmod(q, 4)
             if u < NU and a % MXB == 0:
                 mx(u, list(range(a, a + MXB)))
@@ -325,17 +328,17 @@ def tile_lstmcell2_t_kernel(tc, x, h, c, W, b, gn_weight, gn_bias, out_0, out_1)
             if 0 <= u < NU:
                 tf(u, a)
             s, r = divmod(q - L_D, 16)
-            if 0 <= s < S:
+            if 0 <= s < S and r % 4 < 3:
                 d(s, r // 4, r % 4)
-            s, r = divmod(q - L_D - 3 - L_H, 16)
+            s, r = divmod(q - L_D2, 16)
+            if 0 <= s < S and r % 4 == 0:
+                dso(s, r // 4)
+            s, r = divmod(q - L_D2 - L_H, 16)
             if 0 <= s < S and r % 4 == 0:
                 dh(s, r // 4)
             u, a = divmod(q - L_SQ, 4)
             if 0 <= u < NU:
                 sq(u, a)
-            u, a = divmod(q - L_VE, 4)
-            if 0 <= u < NU and a == 0:
-                var_eps(u)
             u, a = divmod(q - L_P3, 4)
             if 0 <= u < NU:
                 p3(u, a)

@@ -25,12 +25,12 @@ FUNCS = [ACT.Sigmoid, ACT.Sigmoid, ACT.Sigmoid, ACT.Tanh]
 FLOPS = 2 * B * G * H * H
 BYTES = 2 * (2 * B * H + G * H * H + 3 * G * H) + 4 * 2 * B * H
 
-L_SQ = 4
-L_P3 = 10
-L_TF = 15
+L_SQ = 2
+L_P3 = 6
+L_TF = 13
 L_P2 = 8
-L_D = 28
-L_D2 = 33
+L_D = 26
+L_D2 = 31
 L_H = 1
 MXB = 2
 DUP = ()
@@ -197,12 +197,6 @@ def tile_lstmcell2_t_kernel(tc, x, h, c, W, b, gn_weight, gn_bias, out_0, out_1)
                     op1=ALU.add,
                     accum_out=s1[u][:, a : a + 1],
                 )
-            if tiles[-1] == A - 1:
-                t2 = small.tile([P, A], F32, tag="nm")
-                nm[u] = t2
-                nc.vector.tensor_scalar(
-                    out=t2[:], in0=s1[u][:], scalar1=-1.0 / H, scalar2=None, op0=ALU.mult
-                )
 
         def sq(u, a):
             if a == 0:
@@ -213,15 +207,19 @@ def tile_lstmcell2_t_kernel(tc, x, h, c, W, b, gn_weight, gn_bias, out_0, out_1)
                 out=junk[:],
                 in_=lin[u][:, a, :],
                 func=ACT.Square,
-                bias=nm[u][:, a : a + 1],
+                scale=-1.0 * H,
+                bias=s1[u][:, a : a + 1],
                 accum_out=s2[u][:, a : a + 1],
             )
             if a == A - 1:
                 t4 = small.tile([P, A], F32, tag="ve")
                 ve[u] = t4
                 nc.scalar.activation(
-                    out=t4[:], in_=s2[u][:], func=ACT.Identity, scale=1.0 / H, bias=eps_t[:]
+                    out=t4[:], in_=s2[u][:], func=ACT.Identity, scale=1.0 / (H * H * H), bias=eps_t[:]
                 )
+                t2 = small.tile([P, A], F32, tag="nm")
+                nm[u] = t2
+                nc.scalar.activation(out=t2[:], in_=s1[u][:], func=ACT.Copy, scale=-1.0 / H)
 
         def p3(u, a):
             if a == 0:
@@ -256,9 +254,9 @@ def tile_lstmcell2_t_kernel(tc, x, h, c, W, b, gn_weight, gn_bias, out_0, out_1)
                 bias=gwb[:, 16 + jb : 17 + jb],
             )
 
-        def p2(s, j):
-            gi = gT[G * s][:, j, :]
-            gg = gT[G * s + 1][:, j, :]
+        def p2(s):
+            gi = gT[G * s][:]
+            gg = gT[G * s + 1][:]
             nc.vector.tensor_tensor(out=gi, in0=gi, in1=gg, op=ALU.mult)
 
         def back(src, a):
@@ -343,5 +341,5 @@ def tile_lstmcell2_t_kernel(tc, x, h, c, W, b, gn_weight, gn_bias, out_0, out_1)
             if 0 <= u < NU:
                 p3(u, a)
             s, r = divmod(q - L_TF - L_P2, 16)
-            if 0 <= s < S and r < 4:
-                p2(s, r)
+            if 0 <= s < S and r == 0:
+                p2(s)

@@ -70,8 +70,6 @@ def tile_lstmcell2_t_kernel(tc, x, h, c, W, b, gn_weight, gn_bias, out_0, out_1)
         make_identity(nc, ident[:])
         negh = const.tile([P, A], F32)
         nc.vector.memset(negh[:], -0.5)
-        eps_t = const.tile([P, 1], F32)
-        nc.vector.memset(eps_t[:], EPS)
 
         w_codes = const.tile([P, G * H], U32, align_bytes=64)
         w_scales = const.tile([P, G * H], U8, align_bytes=64)
@@ -162,6 +160,11 @@ def tile_lstmcell2_t_kernel(tc, x, h, c, W, b, gn_weight, gn_bias, out_0, out_1)
         rstd = {}
         gT = {}
         fin = {}
+        bst = {}
+        mv = {}
+
+        def stats_on_vector(u):
+            return u % 8 == 7
 
         def mx(u, tiles):
             s = u // G
@@ -170,8 +173,6 @@ def tile_lstmcell2_t_kernel(tc, x, h, c, W, b, gn_weight, gn_bias, out_0, out_1)
             if tiles[0] == 0:
                 lt = linp.tile([P, A, H], F32, tag="lin")
                 lin[u] = lt
-                t1 = small.tile([P, A], F32, tag="s1")
-                s1[u] = t1
             banks = []
             for a in tiles:
                 rows = slice(a * P, (a + 1) * P)
@@ -187,18 +188,36 @@ def tile_lstmcell2_t_kernel(tc, x, h, c, W, b, gn_weight, gn_bias, out_0, out_1)
                         start=True,
                         stop=True,
                     )
-            for a, y in zip(tiles, banks):
-                nc.vector.scalar_tensor_tensor(
-                    out=lin[u][:, a, :],
-                    in0=y[:],
-                    scalar=1.0,
-                    in1=b_bc[:, gc],
-                    op0=ALU.mult,
-                    op1=ALU.add,
-                    accum_out=s1[u][:, a : a + 1],
-                )
+            if stats_on_vector(u):
+                if tiles[0] == 0:
+                    t6 = small.tile([P, A, 6], F32, tag="bst")
+                    bst[u] = t6
+                    t7 = small.tile([P, A, 2], F32, tag="mv")
+                    mv[u] = t7
+                for a, y in zip(tiles, banks):
+                    nc.vector.tensor_tensor(out=lin[u][:, a, :], in0=y[:], in1=b_bc[:, gc], op=ALU.add)
+                for a in tiles:
+                    nc.vector.bn_stats(out=bst[u][:, a, :], in_=lin[u][:, a, :])
+                for a in tiles:
+                    nc.vector.bn_aggr(out=mv[u][:, a, :], in_=bst[u][:, a, :])
+            else:
+                if tiles[0] == 0:
+                    t1 = small.tile([P, A], F32, tag="s1")
+                    s1[u] = t1
+                for a, y in zip(tiles, banks):
+                    nc.vector.scalar_tensor_tensor(
+                        out=lin[u][:, a, :],
+                        in0=y[:],
+                        scalar=1.0,
+                        in1=b_bc[:, gc],
+                        op0=ALU.mult,
+                        op1=ALU.add,
+                        accum_out=s1[u][:, a : a + 1],
+                    )
 
         def sq(u, a):
+            if stats_on_vector(u):
+                return
             if a == 0:
                 t3 = small.tile([P, A], F32, tag="s2")
                 s2[u] = t3
@@ -211,18 +230,25 @@ def tile_lstmcell2_t_kernel(tc, x, h, c, W, b, gn_weight, gn_bias, out_0, out_1)
                 bias=s1[u][:, a : a + 1],
                 accum_out=s2[u][:, a : a + 1],
             )
-            if a == A - 1:
-                t4 = small.tile([P, A], F32, tag="ve")
-                ve[u] = t4
-                nc.scalar.activation(
-                    out=t4[:], in_=s2[u][:], func=ACT.Identity, scale=1.0 / (H * H * H), bias=eps_t[:]
-                )
-                t2 = small.tile([P, A], F32, tag="nm")
-                nm[u] = t2
-                nc.scalar.activation(out=t2[:], in_=s1[u][:], func=ACT.Copy, scale=-1.0 / H)
 
         def p3(u, a):
             if a == 0:
+                if stats_on_vector(u):
+                    sums, c_sum = mv[u][:, :, 0], -1.0
+                    squares, c_sq = mv[u][:, :, 1], 1.0
+                else:
+                    sums, c_sum = s1[u][:], -1.0 / H
+                    squares, c_sq = s2[u][:], 1.0 / (H * H * H)
+                t2 = small.tile([P, A], F32, tag="nm")
+                nm[u] = t2
+                nc.gpsimd.tensor_scalar(
+                    out=t2[:], in0=sums, scalar1=c_sum, scalar2=0.0, op0=ALU.mult, op1=ALU.add
+                )
+                t4 = small.tile([P, A], F32, tag="ve")
+                ve[u] = t4
+                nc.gpsimd.tensor_scalar(
+                    out=t4[:], in0=squares, scalar1=c_sq, scalar2=EPS, op0=ALU.mult, op1=ALU.add
+                )
                 t5 = small.tile([P, A], F32, tag="rstd")
                 rstd[u] = t5
                 nc.gpsimd.tensor_tensor(out=t5[:], in0=ve[u][:], in1=negh[:], op=ALU.pow)

@@ -25,15 +25,15 @@ FUNCS = [ACT.Sigmoid, ACT.Sigmoid, ACT.Sigmoid, ACT.Tanh]
 FLOPS = 2 * B * G * H * H
 BYTES = 2 * (2 * B * H + G * H * H + 3 * G * H) + 4 * 2 * B * H
 
-L_SQ = 2
-L_P3 = 6
-L_TF = 13
+L_SQ = 4
+L_P3 = 10
+L_TF = 15
 L_P2 = 8
-L_D = 26
-L_D2 = 31
+L_D = 28
+L_D2 = 33
 L_H = 1
 MXB = 2
-DUP = ()
+DUP = (0, 1, 2, 3)
 
 
 def tile_lstmcell2_t_kernel(tc, x, h, c, W, b, gn_weight, gn_bias, out_0, out_1):
@@ -200,6 +200,7 @@ def tile_lstmcell2_t_kernel(tc, x, h, c, W, b, gn_weight, gn_bias, out_0, out_1)
                     nc.vector.bn_stats(out=bst[u][:, a, :], in_=lin[u][:, a, :])
                 for a in tiles:
                     nc.vector.bn_aggr(out=mv[u][:, a, :], in_=bst[u][:, a, :])
+                sums, c_sum = mv[u][:, :, 0], -1.0
             else:
                 if tiles[0] == 0:
                     t1 = small.tile([P, A], F32, tag="s1")
@@ -214,6 +215,11 @@ def tile_lstmcell2_t_kernel(tc, x, h, c, W, b, gn_weight, gn_bias, out_0, out_1)
                         op1=ALU.add,
                         accum_out=s1[u][:, a : a + 1],
                     )
+                sums, c_sum = s1[u][:], -1.0 / H
+            if tiles[-1] == A - 1:
+                t2 = small.tile([P, A], F32, tag="nm")
+                nm[u] = t2
+                nc.vector.tensor_scalar(out=t2[:], in0=sums, scalar1=c_sum, scalar2=None, op0=ALU.mult)
 
         def sq(u, a):
             if stats_on_vector(u):
@@ -226,24 +232,16 @@ def tile_lstmcell2_t_kernel(tc, x, h, c, W, b, gn_weight, gn_bias, out_0, out_1)
                 out=junk[:],
                 in_=lin[u][:, a, :],
                 func=ACT.Square,
-                scale=-1.0 * H,
-                bias=s1[u][:, a : a + 1],
+                bias=nm[u][:, a : a + 1],
                 accum_out=s2[u][:, a : a + 1],
             )
 
         def p3(u, a):
             if a == 0:
                 if stats_on_vector(u):
-                    sums, c_sum = mv[u][:, :, 0], -1.0
                     squares, c_sq = mv[u][:, :, 1], 1.0
                 else:
-                    sums, c_sum = s1[u][:], -1.0 / H
-                    squares, c_sq = s2[u][:], 1.0 / (H * H * H)
-                t2 = small.tile([P, A], F32, tag="nm")
-                nm[u] = t2
-                nc.gpsimd.tensor_scalar(
-                    out=t2[:], in0=sums, scalar1=c_sum, scalar2=0.0, op0=ALU.mult, op1=ALU.add
-                )
+                    squares, c_sq = s2[u][:], 1.0 / H
                 t4 = small.tile([P, A], F32, tag="ve")
                 ve[u] = t4
                 nc.gpsimd.tensor_scalar(
@@ -280,9 +278,9 @@ def tile_lstmcell2_t_kernel(tc, x, h, c, W, b, gn_weight, gn_bias, out_0, out_1)
                 bias=gwb[:, 16 + jb : 17 + jb],
             )
 
-        def p2(s):
-            gi = gT[G * s][:]
-            gg = gT[G * s + 1][:]
+        def p2(s, j):
+            gi = gT[G * s][:, j, :]
+            gg = gT[G * s + 1][:, j, :]
             nc.vector.tensor_tensor(out=gi, in0=gi, in1=gg, op=ALU.mult)
 
         def back(src, a):
@@ -367,5 +365,5 @@ def tile_lstmcell2_t_kernel(tc, x, h, c, W, b, gn_weight, gn_bias, out_0, out_1)
             if 0 <= u < NU:
                 p3(u, a)
             s, r = divmod(q - L_TF - L_P2, 16)
-            if 0 <= s < S and r == 0:
-                p2(s)
+            if 0 <= s < S and r < 4:
+                p2(s, r)

@@ -33,7 +33,7 @@ L_D = 28
 L_D2 = 33
 L_H = 1
 MXB = 2
-DUP = (0, 1, 2, 3)
+DUP = ()
 
 
 def tile_lstmcell2_t_kernel(tc, x, h, c, W, b, gn_weight, gn_bias, out_0, out_1):
@@ -70,6 +70,8 @@ def tile_lstmcell2_t_kernel(tc, x, h, c, W, b, gn_weight, gn_bias, out_0, out_1)
         make_identity(nc, ident[:])
         negh = const.tile([P, A], F32)
         nc.vector.memset(negh[:], -0.5)
+        eps_t = const.tile([P, 1], F32)
+        nc.vector.memset(eps_t[:], EPS)
 
         w_codes = const.tile([P, G * H], U32, align_bytes=64)
         w_scales = const.tile([P, G * H], U8, align_bytes=64)
@@ -118,7 +120,7 @@ def tile_lstmcell2_t_kernel(tc, x, h, c, W, b, gn_weight, gn_bias, out_0, out_1)
 
         def prep_h(s):
             hg = hq.tile([P, A * P * 4], BF16, tag="h_grouped", align_bytes=64)
-            words_to_grouped(h_raw[s][:], hg[:], A, ["v"])
+            words_to_grouped(h_raw[s][:], hg[:], A, ["v", "s"])
             hc = hq.tile([P, A * P], U32, tag="h_codes", align_bytes=64)
             hs = hq.tile([P, A * P], U8, tag="h_scales", align_bytes=64)
             nc.vector.quantize_mx(out=hc[:].bitcast(FP8X4), scales=hs[:], in_=hg[:])
@@ -160,11 +162,6 @@ def tile_lstmcell2_t_kernel(tc, x, h, c, W, b, gn_weight, gn_bias, out_0, out_1)
         rstd = {}
         gT = {}
         fin = {}
-        bst = {}
-        mv = {}
-
-        def stats_on_vector(u):
-            return u % 8 == 7
 
         def mx(u, tiles):
             s = u // G
@@ -173,6 +170,8 @@ def tile_lstmcell2_t_kernel(tc, x, h, c, W, b, gn_weight, gn_bias, out_0, out_1)
             if tiles[0] == 0:
                 lt = linp.tile([P, A, H], F32, tag="lin")
                 lin[u] = lt
+                t1 = small.tile([P, A], F32, tag="s1")
+                s1[u] = t1
             banks = []
             for a in tiles:
                 rows = slice(a * P, (a + 1) * P)
@@ -188,42 +187,18 @@ def tile_lstmcell2_t_kernel(tc, x, h, c, W, b, gn_weight, gn_bias, out_0, out_1)
                         start=True,
                         stop=True,
                     )
-            if stats_on_vector(u):
-                if tiles[0] == 0:
-                    t6 = small.tile([P, A, 6], F32, tag="bst")
-                    bst[u] = t6
-                    t7 = small.tile([P, A, 2], F32, tag="mv")
-                    mv[u] = t7
-                for a, y in zip(tiles, banks):
-                    nc.vector.tensor_tensor(out=lin[u][:, a, :], in0=y[:], in1=b_bc[:, gc], op=ALU.add)
-                for a in tiles:
-                    nc.vector.bn_stats(out=bst[u][:, a, :], in_=lin[u][:, a, :])
-                for a in tiles:
-                    nc.vector.bn_aggr(out=mv[u][:, a, :], in_=bst[u][:, a, :])
-                sums, c_sum = mv[u][:, :, 0], -1.0
-            else:
-                if tiles[0] == 0:
-                    t1 = small.tile([P, A], F32, tag="s1")
-                    s1[u] = t1
-                for a, y in zip(tiles, banks):
-                    nc.vector.scalar_tensor_tensor(
-                        out=lin[u][:, a, :],
-                        in0=y[:],
-                        scalar=1.0,
-                        in1=b_bc[:, gc],
-                        op0=ALU.mult,
-                        op1=ALU.add,
-                        accum_out=s1[u][:, a : a + 1],
-                    )
-                sums, c_sum = s1[u][:], -1.0 / H
-            if tiles[-1] == A - 1:
-                t2 = small.tile([P, A], F32, tag="nm")
-                nm[u] = t2
-                nc.vector.tensor_scalar(out=t2[:], in0=sums, scalar1=c_sum, scalar2=None, op0=ALU.mult)
+            for a, y in zip(tiles, banks):
+                nc.vector.scalar_tensor_tensor(
+                    out=lin[u][:, a, :],
+                    in0=y[:],
+                    scalar=1.0,
+                    in1=b_bc[:, gc],
+                    op0=ALU.mult,
+                    op1=ALU.add,
+                    accum_out=s1[u][:, a : a + 1],
+                )
 
         def sq(u, a):
-            if stats_on_vector(u):
-                return
             if a == 0:
                 t3 = small.tile([P, A], F32, tag="s2")
                 s2[u] = t3
@@ -232,20 +207,23 @@ def tile_lstmcell2_t_kernel(tc, x, h, c, W, b, gn_weight, gn_bias, out_0, out_1)
                 out=junk[:],
                 in_=lin[u][:, a, :],
                 func=ACT.Square,
-                bias=nm[u][:, a : a + 1],
+                scale=-1.0 * H,
+                bias=s1[u][:, a : a + 1],
                 accum_out=s2[u][:, a : a + 1],
             )
+            if a == A - 1:
+                t4 = small.tile([P, A], F32, tag="ve")
+                ve[u] = t4
+                nc.scalar.activation(
+                    out=t4[:], in_=s2[u][:], func=ACT.Identity, scale=1.0 / (H * H * H), bias=eps_t[:]
+                )
 
         def p3(u, a):
             if a == 0:
-                if stats_on_vector(u):
-                    squares, c_sq = mv[u][:, :, 1], 1.0
-                else:
-                    squares, c_sq = s2[u][:], 1.0 / H
-                t4 = small.tile([P, A], F32, tag="ve")
-                ve[u] = t4
+                t2 = small.tile([P, A], F32, tag="nm")
+                nm[u] = t2
                 nc.gpsimd.tensor_scalar(
-                    out=t4[:], in0=squares, scalar1=c_sq, scalar2=EPS, op0=ALU.mult, op1=ALU.add
+                    out=t2[:], in0=s1[u][:], scalar1=-1.0 / H, scalar2=0.0, op0=ALU.mult, op1=ALU.add
                 )
                 t5 = small.tile([P, A], F32, tag="rstd")
                 rstd[u] = t5
@@ -281,7 +259,10 @@ def tile_lstmcell2_t_kernel(tc, x, h, c, W, b, gn_weight, gn_bias, out_0, out_1)
         def p2(s, j):
             gi = gT[G * s][:, j, :]
             gg = gT[G * s + 1][:, j, :]
-            nc.vector.tensor_tensor(out=gi, in0=gi, in1=gg, op=ALU.mult)
+            if j >= 2:
+                nc.gpsimd.tensor_tensor(out=gi, in0=gi, in1=gg, op=ALU.mult)
+            else:
+                nc.vector.tensor_tensor(out=gi, in0=gi, in1=gg, op=ALU.mult)
 
         def back(src, a):
             bk = ps_k.tile([P, H], F32, tag="bk")

from contextlib import ExitStack

import concourse.mybir as mybir
from concourse.masks import make_identity

F32 = mybir.dt.float32
BF16 = mybir.dt.bfloat16
U32 = mybir.dt.uint32
U8 = mybir.dt.uint8
FP8X4 = mybir.dt.float8_e4m3fn_x4
ALU = mybir.AluOpType
ACT = mybir.ActivationFunctionType

P = 128
B = 4096
H = 512
G = 4
EPS = 1e-5
A = 4
S = B // (A * P)
NU = S * G
GATE_ORDER = [0, 3, 1, 2]
FUNCS = [ACT.Sigmoid, ACT.Sigmoid, ACT.Sigmoid, ACT.Tanh]

FLOPS = 2 * B * G * H * H
BYTES = 2 * (2 * B * H + G * H * H + 3 * G * H) + 4 * 2 * B * H

L_SQ = 4
L_P3 = 10
L_TF = 15
L_P2 = 8
L_D = 28
L_D2 = 33
L_H = 1
MXB = 2
DUP = ()


def tile_lstmcell2_t_kernel(tc, x, h, c, W, b, gn_weight, gn_bias, out_0, out_1):
    nc = tc.nc
    h_v = h.rearrange("(s p a) k -> s p (a k)", p=P, a=A)
    c_v = c.rearrange("(s p a) k -> s p (a k)", p=P, a=A)
    ho_v = out_0.rearrange("(s p a) k -> s p (a k)", p=P, a=A)
    co_v = out_1.rearrange("(s p a) k -> s p (a k)", p=P, a=A)
    w_v = W.rearrange("(g t p) k -> g p t k", p=P, t=4)

    with ExitStack() as ctx:
        ctx.enter_context(tc.manual_schedule())
        const = ctx.enter_context(tc.tile_pool(name="const", bufs=1))
        ps_y = ctx.enter_context(tc.psum_pool(name="ps_y", bufs=2))
        ps_n = ctx.enter_context(tc.psum_pool(name="ps_n", bufs=3))
        ps_k = ctx.enter_context(tc.psum_pool(name="ps_k", bufs=3))
        hin = ctx.enter_context(tc.tile_pool(name="hin", bufs=2))
        cin = ctx.enter_context(tc.tile_pool(name="cin", bufs=3))
        hq = ctx.enter_context(tc.tile_pool(name="hq", bufs=2))
        wraw = ctx.enter_context(tc.tile_pool(name="wraw", bufs=4))
        wgrp = ctx.enter_context(tc.tile_pool(name="wgrp", bufs=2))
        work = ctx.enter_context(tc.tile_pool(name="work", bufs=3))
        linp = ctx.enter_context(tc.tile_pool(name="linp", bufs=5))
        gtp = ctx.enter_context(tc.tile_pool(name="gtp", bufs=7))
        small = ctx.enter_context(tc.tile_pool(name="small", bufs=8))
        outp = ctx.enter_context(tc.tile_pool(name="outp", bufs=2))

        warm = const.tile([P, 1], F32)
        nc.vector.memset(warm[:], 0.0)
        warm2 = const.tile([P, 1], F32)
        nc.scalar.activation(out=warm2[:], in_=warm[:], func=ACT.Sigmoid)

        ident = const.tile([P, P], F32)
        make_identity(nc, ident[:])
        negh = const.tile([P, A], F32)
        nc.vector.memset(negh[:], -0.5)
        eps_t = const.tile([P, 1], F32)
        nc.vector.memset(eps_t[:], EPS)

        w_codes = const.tile([P, G * H], U32, align_bytes=64)
        w_scales = const.tile([P, G * H], U8, align_bytes=64)
        b_bc = const.tile([P, G * H], BF16)
        gwb = const.tile([P, 32], F32)
        rows16 = const.tile([P, P], BF16)
        rows32 = const.tile([P, P], F32)

        h_raw = {}
        c_raw = {}
        w_raw = {}
        h_codes = {}
        h_scales = {}

        def load(s):
            hr = hin.tile([P, A * H], BF16, tag="h_raw")
            nc.sync.dma_start(out=hr[:], in_=h_v[s])
            h_raw[s] = hr

        def load_c(s):
            cr = cin.tile([P, A * H], BF16, tag="c_raw")
            nc.sync.dma_start(out=cr[:], in_=c_v[s])
            c_raw[s] = cr

        def load_w(g):
            wr = wraw.tile([P, 4 * H], BF16, tag="w_raw")
            nc.sync.dma_start(out=wr[:].rearrange("p (t k) -> p t k", k=H), in_=w_v[g])
            w_raw[g] = wr

        def words_to_grouped(raw, grouped, n_tiles, engines):
            g32 = grouped.bitcast(F32).rearrange("p (a c u) -> p a c u", c=P, u=2)
            for pair in range(n_tiles // 2):
                xt = ps_n.tile([P, H], F32, tag="nT")
                xv = xt[:].rearrange("p (a u c) -> p a u c", a=2, u=2)
                for a in range(2):
                    t = 2 * pair + a
                    words = raw[:, t * H : (t + 1) * H].bitcast(F32)
                    for u in range(2):
                        nc.tensor.transpose(xv[:, a, u, :], words[:, u * P : (u + 1) * P], ident[:])
                src = xt[:].rearrange("p (a u c) -> p a c u", a=2, u=2)
                dst = g32[:, 2 * pair : 2 * pair + 2, :, :]
                if engines[pair % len(engines)] == "v":
                    nc.vector.tensor_copy(out=dst, in_=src)
                else:
                    nc.scalar.copy(out=dst, in_=src)

        def prep_h(s):
            hg = hq.tile([P, A * P * 4], BF16, tag="h_grouped", align_bytes=64)
            words_to_grouped(h_raw[s][:], hg[:], A, ["v", "s"])
            hc = hq.tile([P, A * P], U32, tag="h_codes", align_bytes=64)
            hs = hq.tile([P, A * P], U8, tag="h_scales", align_bytes=64)
            nc.vector.quantize_mx(out=hc[:].bitcast(FP8X4), scales=hs[:], in_=hg[:])
            h_codes[s] = hc
            h_scales[s] = hs

        def prep_w(g):
            wg = wgrp.tile([P, H * 4], BF16, tag="w_grouped", align_bytes=64)
            words_to_grouped(w_raw[g][:], wg[:], 4, ["v", "s"])
            nc.vector.quantize_mx(
                out=w_codes[:, g * H : (g + 1) * H].bitcast(FP8X4),
                scales=w_scales[:, g * H : (g + 1) * H],
                in_=wg[:],
            )

        def prep_gwb():
            nc.vector.tensor_copy(out=rows32[:], in_=rows16[:])
            colsT = ps_n.tile([P, H], F32, tag="nT")
            nc.tensor.transpose(colsT[:, 0:P], rows32[:], ident[:])
            nc.vector.tensor_copy(out=gwb[:], in_=colsT[:, 0:32])

        nc.vector.memset(rows16[:], 0.0)
        load(0)
        load_w(GATE_ORDER[0])
        nc.scalar.dma_start(out=b_bc[:], in_=b.partition_broadcast(P))
        nc.scalar.dma_start(out=rows16[0:16, :], in_=gn_weight.rearrange("(j c) -> j c", c=P))
        nc.scalar.dma_start(out=rows16[16:32, :], in_=gn_bias.rearrange("(j c) -> j c", c=P))
        for g in GATE_ORDER[1:]:
            load_w(g)
        load(1)
        prep_h(0)
        prep_w(GATE_ORDER[0])

        lin = {}
        s1 = {}
        nm = {}
        s2 = {}
        ve = {}
        rstd = {}
        gT = {}
        fin = {}

        def mx(u, tiles):
            s = u // G
            g = GATE_ORDER[u % G]
            gc = slice(g * H, (g + 1) * H)
            if tiles[0] == 0:
                lt = linp.tile([P, A, H], F32, tag="lin")
                lin[u] = lt
                t1 = small.tile([P, A], F32, tag="s1")
                s1[u] = t1
            banks = []
            for a in tiles:
                rows = slice(a * P, (a + 1) * P)
                y = ps_y.tile([P, H], F32, tag="y")
                banks.append(y)
                for rep in range(2 if a in DUP else 1):
                    nc.tensor.matmul_mx(
                        out=y[:],
                        lhsT=h_codes[s][:, rows].bitcast(FP8X4),
                        lhsT_scale=h_scales[s][:, rows],
                        rhs=w_codes[:, gc].bitcast(FP8X4),
                        rhs_scale=w_scales[:, gc],
                        start=True,
                        stop=True,
                    )
            for a, y in zip(tiles, banks):
                nc.vector.scalar_tensor_tensor(
                    out=lin[u][:, a, :],
                    in0=y[:],
                    scalar=1.0,
                    in1=b_bc[:, gc],
                    op0=ALU.mult,
                    op1=ALU.add,
                    accum_out=s1[u][:, a : a + 1],
                )

        def sq(u, a):
            if a == 0:
                t3 = small.tile([P, A], F32, tag="s2")
                s2[u] = t3
            junk = work.tile([P, H], F32, tag="junk")
            nc.scalar.activation(
                out=junk[:],
                in_=lin[u][:, a, :],
                func=ACT.Square,
                scale=-1.0 * H,
                bias=s1[u][:, a : a + 1],
                accum_out=s2[u][:, a : a + 1],
            )
            if a == A - 1:
                t4 = small.tile([P, A], F32, tag="ve")
                ve[u] = t4
                nc.scalar.activation(
                    out=t4[:], in_=s2[u][:], func=ACT.Identity, scale=1.0 / (H * H * H), bias=eps_t[:]
                )

        def p3(u, a):
            if a == 0:
                t2 = small.tile([P, A], F32, tag="nm")
                nm[u] = t2
                nc.gpsimd.tensor_scalar(
                    out=t2[:], in0=s1[u][:], scalar1=-1.0 / H, scalar2=0.0, op0=ALU.mult, op1=ALU.add
                )
                t5 = small.tile([P, A], F32, tag="rstd")
                rstd[u] = t5
                nc.gpsimd.tensor_tensor(out=t5[:], in0=ve[u][:], in1=negh[:], op=ALU.pow)
            nc.gpsimd.tensor_scalar(
                out=lin[u][:, a, :],
                in0=lin[u][:, a, :],
                scalar1=nm[u][:, a : a + 1],
                scalar2=rstd[u][:, a : a + 1],
                op0=ALU.add,
                op1=ALU.mult,
            )

        def tf(u, j):
            g = GATE_ORDER[u % G]
            if j == 0:
                gt = gtp.tile([P, 4, A * P], F32, tag="gT")
                gT[u] = gt
            nT = ps_n.tile([P, H], F32, tag="nT")
            for a in range(A):
                nc.tensor.transpose(
                    nT[:, a * P : (a + 1) * P], lin[u][:, a, j * P : (j + 1) * P], ident[:]
                )
            jb = g * 4 + j
            nc.scalar.activation(
                out=gT[u][:, j, :],
                in_=nT[:],
                func=FUNCS[g],
                scale=gwb[:, jb : jb + 1],
                bias=gwb[:, 16 + jb : 17 + jb],
            )

        def p2(s, j):
            gi = gT[G * s][:, j, :]
            gg = gT[G * s + 1][:, j, :]
            if j >= 2:
                nc.gpsimd.tensor_tensor(out=gi, in0=gi, in1=gg, op=ALU.mult)
            else:
                nc.vector.tensor_tensor(out=gi, in0=gi, in1=gg, op=ALU.mult)

        def back(src, a):
            bk = ps_k.tile([P, H], F32, tag="bk")
            for j in range(4):
                nc.tensor.transpose(
                    bk[:, j * P : (j + 1) * P], src[:, j, a * P : (a + 1) * P], ident[:]
                )
            return bk

        def d(s, a, k):
            cols = slice(a * H, (a + 1) * H)
            if k == 0:
                if a == 0:
                    co = outp.tile([P, A * H], F32, tag="c_out")
                    fin["c_out"] = co
                sf = back(gT[G * s + 2], a)
                p1 = work.tile([P, H], F32, tag="p1")
                fin["p1"] = p1
                nc.vector.tensor_tensor(out=p1[:], in0=sf[:], in1=c_raw[s][:, cols], op=ALU.mult)
            if k == 1:
                pp = back(gT[G * s], a)
                nc.vector.tensor_tensor(
                    out=fin["c_out"][:, cols], in0=pp[:], in1=fin["p1"][:], op=ALU.add
                )
            if k == 2:
                tcn = work.tile([P, H], F32, tag="tc")
                fin["tc", a] = tcn
                nc.scalar.activation(out=tcn[:], in_=fin["c_out"][:, cols], func=ACT.Tanh)
                if s == S - 1:
                    nc.sync.dma_start(out=co_v[s][:, cols], in_=fin["c_out"][:, cols])
                elif a == A - 1:
                    nc.sync.dma_start(out=co_v[s], in_=fin["c_out"][:])

        def dso(s, a):
            so = back(gT[G * s + 3], a)
            fin["so", a] = so

        def dh(s, a):
            cols = slice(a * H, (a + 1) * H)
            if a == 0:
                ho = outp.tile([P, A * H], F32, tag="h_out")
                fin["h_out"] = ho
            nc.vector.tensor_tensor(
                out=fin["h_out"][:, cols], in0=fin["so", a][:], in1=fin["tc", a][:], op=ALU.mult
            )
            if s == S - 1:
                nc.sync.dma_start(out=ho_v[s][:, cols], in_=fin["h_out"][:, cols])
            elif a == A - 1:
                nc.sync.dma_start(out=ho_v[s], in_=fin["h_out"][:])

        for q in range(16 * S + L_D2 + 24):
            u, a = divmod(q, 4)
            if u < NU and a % MXB == 0:
                mx(u, list(range(a, a + MXB)))
            if q in (1, 5, 9):
                prep_w(GATE_ORDER[q // 4 + 1])
            if q == 11:
                prep_gwb()
            if q % 16 == 10 and q // 16 + 2 < S:
                load(q // 16 + 2)
            if q % 16 == 0 and q // 16 < S:
                load_c(q // 16)
            if q % 16 == 6 and q // 16 + 1 < S:
                prep_h(q // 16 + 1)
            u, a = divmod(q - L_TF, 4)
            if 0 <= u < NU:
                tf(u, a)
            s, r = divmod(q - L_D, 16)
            if 0 <= s < S and r % 4 < 3:
                d(s, r // 4, r % 4)
            s, r = divmod(q - L_D2, 16)
            if 0 <= s < S and r % 4 == 0:
                dso(s, r // 4)
            s, r = divmod(q - L_D2 - L_H, 16)
            if 0 <= s < S and r % 4 == 0:
                dh(s, r // 4)
            u, a = divmod(q - L_SQ, 4)
            if 0 <= u < NU:
                sq(u, a)
            u, a = divmod(q - L_P3, 4)
            if 0 <= u < NU:
                p3(u, a)
            s, r = divmod(q - L_TF - L_P2, 16)
            if 0 <= s < S and r < 4:
                p2(s, r)
